import numpy as np
import ml_dtypes


def mxq(x, axis, fmt="e4m3"):
    dtype, down = {"e4m3": (ml_dtypes.float8_e4m3fn, 7), "e5m2": (ml_dtypes.float8_e5m2, 14)}[fmt]
    v = np.moveaxis(np.asarray(x, np.float32).astype(ml_dtypes.bfloat16).astype(np.float64), axis, -1)
    blocks = v.reshape(v.shape[:-1] + (-1, 32))
    amax = np.abs(blocks).max(-1, keepdims=True)
    byte = np.maximum(np.where(amax > 0, np.frexp(amax)[1] - 1 + 127, 0) - down, 1)
    scale = np.exp2(byte - 127.0)
    codes = (blocks / scale).astype(np.float32).astype(dtype).astype(np.float64)
    return np.moveaxis((codes * scale).reshape(v.shape), -1, axis)


WIDE = False


def mx_kscale(k):
    if not WIDE:
        return np.ones(k)
    levels = np.array([10, -10, 5, -5, 0])
    if k % 512:
        return np.exp2(np.random.permutation(np.resize(levels, k // 32))).repeat(32)
    a = np.empty((k // 512, 16))
    for p in range(k // 512):
        a[p, :8] = np.random.permutation(np.resize(levels, 8))
        for g in range(8):
            far = levels[np.abs(levels - a[p, g]) >= 10]
            a[p, g + 8] = far[np.random.randint(len(far))]
    return np.exp2(a.ravel()).repeat(32)


BF16 = ml_dtypes.bfloat16


def bf(x):
    return np.asarray(x, np.float32).astype(BF16)


def f64(x):
    return np.asarray(x).astype(np.float64)


B, S, C, H, D = 4, 512, 1024, 8, 128
E = H * D
EPS = 1e-15


def setup_inputs():
    t = mx_kscale(E)
    return {"q_feat": bf(np.maximum(np.random.standard_normal((B, H, S, D)), 0.0)),
            "vk": bf(np.random.standard_normal((B, H, D, D)) * np.sqrt(S) * t.reshape(H, D)[None, :, :, None]),
            "k_sum": bf(S * (0.11 + 0.02 * np.random.standard_normal((B, H, D)))),
            "Wo": bf(np.random.standard_normal((C, E)) * 6.0 / np.sqrt(E) / t[None, :]),
            "bo": bf(np.random.standard_normal(C) * 0.1)}


def reference(q_feat, vk, k_sum, Wo, bo):
    hs = f64(vk) @ f64(q_feat).transpose(0, 1, 3, 2)
    den = (f64(q_feat) * f64(k_sum)[:, :, None, :]).sum(-1)
    hs = hs / (den[:, :, None, :] + EPS)
    a = hs.transpose(0, 3, 1, 2).reshape(B, S, E)
    return (mxq(a, 2, "e4m3") @ mxq(f64(Wo), 1, "e4m3").T) + f64(bo)

@@ -1,0 +1,257 @@
+from contextlib import ExitStack
+
+import concourse.mybir as mybir
+from concourse.masks import make_identity
+
+BF16 = mybir.dt.bfloat16
+F32 = mybir.dt.float32
+U32 = mybir.dt.uint32
+U8 = mybir.dt.uint8
+FP8X4 = mybir.dt.float8_e4m3fn_x4
+COPY = mybir.ActivationFunctionType.Copy
+ADD = mybir.AluOpType.add
+MULT = mybir.AluOpType.mult
+
+B, H, S, D, C = 4, 8, 512, 128, 1024
+E = H * D
+EPS = 1e-15
+P = 128
+PACK = 4
+K_PASS = P * PACK
+PASSES = E // K_PASS
+BANK = 512
+CHUNKS = S // P
+UNITS = B * CHUNKS
+C_HALVES = C // BANK
+READ = D + 1
+HEADS_PER_BANK = BANK // READ
+HS_BANKS = -(-H // HEADS_PER_BANK)
+VK_SLOT = 144
+
+FLOPS = 2 * B * S * E * C + 2 * B * H * S * D * (D + 1)
+
+
+def tile_lineartransformerblock_pc_kernel(tc, q_feat, vk, k_sum, Wo, bo, out):
+    nc = tc.nc
+    with ExitStack() as ctx:
+        ctx.enter_context(tc.manual_schedule())
+        keep = ctx.enter_context(tc.tile_pool(name="keep", bufs=1))
+        work = ctx.enter_context(tc.tile_pool(name="work", bufs=3))
+        psum = ctx.enter_context(tc.psum_pool(name="psum", bufs=8))
+
+        vk_sb = []
+        q_sb = []
+        for b in range(B):
+            vk_b = keep.tile([P, H, D], BF16, name="vk%d" % b)
+            q_b = keep.tile([P, H, CHUNKS * D], BF16, name="q%d" % b)
+            vk_sb.append(vk_b)
+            q_sb.append(q_b)
+        wo_sb = keep.tile([P, C // P, E], BF16)
+
+        def load_batch(b):
+            nc.sync.dma_start(out=q_sb[b][:], in_=q_feat[b].rearrange("h (p j) d -> p h (j d)", j=CHUNKS))
+            nc.sync.dma_start(out=vk_sb[b][:], in_=vk[b].rearrange("h n d -> n h d"))
+
+        ks_rows = keep.tile([P, D], BF16)
+        nc.vector.memset(ks_rows[32:64, :], 0.0)
+        nc.vector.memset(ks_rows[64:128, :], 0.0)
+        bo_rows = keep.tile([P, C], BF16)
+        nc.vector.memset(bo_rows[:], 0.0)
+
+        wo_rows = Wo.rearrange("(k p) e -> p k e", p=P)
+        load_batch(0)
+        nc.sync.dma_start(out=ks_rows[0 : B * H, :], in_=k_sum.rearrange("b h d -> (b h) d"))
+        nc.sync.dma_start(out=bo_rows[0:1, :], in_=bo.rearrange("(o c) -> o c", o=1))
+        for half in range(C_HALVES):
+            rows = slice(half * (BANK // P), (half + 1) * (BANK // P))
+            nc.sync.dma_start(out=wo_sb[:, rows, :], in_=wo_rows[:, rows, :])
+        for b in range(1, B):
+            load_batch(b)
+
+        ident_bf = keep.tile([P, P], BF16)
+        make_identity(nc, ident_bf[:])
+        ident_f32 = keep.tile([P, P], F32)
+        make_identity(nc, ident_f32[:])
+        ones = keep.tile([P, P], BF16)
+        nc.vector.memset(ones[:], 1.0)
+
+        bias = keep.tile([P, C], F32)
+
+        def spread_bias():
+            for half in range(C_HALVES):
+                cols = slice(half * BANK, (half + 1) * BANK)
+                spread = psum.tile([P, BANK], F32, tag="bank")
+                nc.tensor.matmul(out=spread[:], lhsT=ones[:], rhs=bo_rows[:, cols], start=True, stop=True)
+                nc.vector.tensor_copy(out=bias[:, cols], in_=spread[:])
+
+        vkT = keep.tile([P, B * H, VK_SLOT], BF16)
+
+        def transpose_k_sum():
+            ksT = psum.tile([P, P], BF16, tag="bank")
+            nc.tensor.transpose(ksT[:], ks_rows[:], ident_bf[:])
+            nc.vector.tensor_copy(out=vkT[:, :, D : D + 1], in_=ksT[:, 0 : B * H].unsqueeze(2))
+
+        def transpose_vk(b):
+            flipped = psum.tile([P, H, D], BF16, tag="bank")
+            for h in range(H):
+                nc.tensor.transpose(flipped[:, h, :], vk_sb[b][:, h, :], ident_bf[:])
+            nc.vector.tensor_copy(out=vkT[:, b * H : (b + 1) * H, 0:D], in_=flipped[:])
+
+        wo_words = wo_sb[:].rearrange("p k e -> p (k e)").bitcast(F32)
+        wo_grouped = keep.tile([P, PASSES * C * PACK], BF16, align_bytes=64)
+        wo_pairs = wo_grouped[:].bitcast(F32).rearrange("p (g c u) -> p g c u", g=PASSES, u=2)
+        wo_codes = keep.tile([P, PASSES * C], U32, align_bytes=64)
+        wo_scales = keep.tile([P, PASSES * C], U8, align_bytes=64)
+
+        def prepare_wo(half, g):
+            for quarter in range(2):
+                c0 = half * BANK + quarter * 2 * P
+                flipped = psum.tile([P, 2, 2 * P], F32, tag="bank")
+                for u in range(2):
+                    for k in range(2):
+                        first = (c0 // P + k) * (E // 2) + 2 * g * P + u
+                        nc.tensor.transpose(
+                            flipped[:, u, k * P : (k + 1) * P],
+                            wo_words[:, first : first + 2 * P - u : 2],
+                            ident_f32[:],
+                        )
+                pairs = wo_pairs[:, g, c0 : c0 + 2 * P, :]
+                if quarter == 0:
+                    nc.scalar.copy(out=pairs, in_=flipped[:].rearrange("p u c -> p c u"))
+                else:
+                    nc.vector.tensor_copy(out=pairs, in_=flipped[:].rearrange("p u c -> p c u"))
+            first = g * C + half * BANK
+            nc.vector.quantize_mx(
+                out=wo_codes[:, first : first + BANK].bitcast(FP8X4),
+                scales=wo_scales[:, first : first + BANK],
+                in_=wo_grouped[:, first * PACK : (first + BANK) * PACK],
+            )
+
+        qT = {}
+        a_rows = {}
+        a_grouped = {}
+        a_codes = {}
+        a_scales = {}
+
+        def transpose_q(u):
+            b, j = divmod(u, CHUNKS)
+            flipped = psum.tile([P, H, P], BF16, tag="bank")
+            for h in range(H):
+                nc.tensor.transpose(flipped[:, h, :], q_sb[b][:, h, j * D : (j + 1) * D], ident_bf[:])
+            qT_u = work.tile([P, H, P], BF16, tag="qT")
+            nc.scalar.copy(out=qT_u[:], in_=flipped[:])
+            qT[u] = qT_u
+
+        def read_out(u):
+            b = u // CHUNKS
+            banks = []
+            for k in range(HS_BANKS):
+                bank = psum.tile([P, BANK], F32, tag="bank")
+                banks.append(bank)
+            for h in range(H):
+                k, slot = divmod(h, HEADS_PER_BANK)
+                nc.tensor.matmul(
+                    out=banks[k][:, slot * READ : (slot + 1) * READ],
+                    lhsT=qT[u][:, h, :],
+                    rhs=vkT[:, b * H + h, 0:READ],
+                    start=True,
+                    stop=True,
+                )
+            den = work.tile([P, H], F32, tag="den")
+            for k in range(HS_BANKS):
+                h0 = k * HEADS_PER_BANK
+                n = min(HEADS_PER_BANK, H - h0)
+                slots = banks[k][:, 0 : n * READ].rearrange("p (k r) -> p k r", r=READ)
+                nc.vector.tensor_scalar_add(out=den[:, h0 : h0 + n].unsqueeze(2), in0=slots[:, :, D:READ], scalar1=EPS)
+            rden = work.tile([P, H], F32, tag="rden")
+            nc.vector.reciprocal(out=rden[:], in_=den[:])
+            a_u = work.tile([P, E], BF16, tag="a")
+            first_heads = banks[0][:, 0 : HEADS_PER_BANK * READ].rearrange("p (k r) -> p k r", r=READ)
+            nc.vector.tensor_tensor(
+                out=a_u[:, 0 : HEADS_PER_BANK * D].rearrange("p (k n) -> p k n", n=D),
+                in0=first_heads[:, :, 0:D],
+                in1=rden[:, 0:HEADS_PER_BANK].unsqueeze(2).to_broadcast([P, HEADS_PER_BANK, D]),
+                op=MULT,
+            )
+            for h in range(HEADS_PER_BANK, H):
+                k, slot = divmod(h, HEADS_PER_BANK)
+                nc.scalar.activation(
+                    out=a_u[:, h * D : (h + 1) * D],
+                    in_=banks[k][:, slot * READ : slot * READ + D],
+                    func=COPY,
+                    scale=rden[:, h : h + 1],
+                )
+            a_rows[u] = a_u
+
+        def transpose_a(u):
+            words = a_rows[u][:].bitcast(F32)
+            flipped = psum.tile([P, BANK], F32, tag="bank")
+            for w in range(E // 2 // P):
+                first = (w // 2) * 2 * P + w % 2
+                nc.tensor.transpose(
+                    flipped[:, w * P : (w + 1) * P], words[:, first : first + 2 * P - w % 2 : 2], ident_f32[:]
+                )
+            grouped = work.tile([P, E], BF16, tag="grouped", align_bytes=64)
+            nc.scalar.copy(
+                out=grouped[:].bitcast(F32).rearrange("p (g s u) -> p g s u", g=PASSES, u=2),
+                in_=flipped[:].rearrange("p (g u s) -> p g s u", g=PASSES, u=2),
+            )
+            a_grouped[u] = grouped
+
+        def quantise_a(u):
+            codes = work.tile([P, PASSES * P], U32, tag="codes", bufs=6, align_bytes=64)
+            scales = work.tile([P, PASSES * P], U8, tag="scales", bufs=6, align_bytes=64)
+            nc.vector.quantize_mx(out=codes[:].bitcast(FP8X4), scales=scales[:], in_=a_grouped[u][:])
+            a_codes[u] = codes
+            a_scales[u] = scales
+
+        def project(u):
+            b, j = divmod(u, CHUNKS)
+            rows = out[b].rearrange("(p j) c -> p j c", j=CHUNKS)
+            for half in range(C_HALVES):
+                acc = psum.tile([P, BANK], F32, tag="bank")
+                for g in range(PASSES):
+                    tokens = slice(g * P, (g + 1) * P)
+                    cols = slice(g * C + half * BANK, g * C + (half + 1) * BANK)
+                    nc.tensor.matmul_mx(
+                        out=acc[:],
+                        lhsT=a_codes[u][:, tokens].bitcast(FP8X4),
+                        lhsT_scale=a_scales[u][:, tokens],
+                        rhs=wo_codes[:, cols].bitcast(FP8X4),
+                        rhs_scale=wo_scales[:, cols],
+                        start=(g == 0),
+                        stop=(g == PASSES - 1),
+                    )
+                cols = slice(half * BANK, (half + 1) * BANK)
+                res = work.tile([P, BANK], F32, tag="res", bufs=6)
+                nc.vector.tensor_tensor(out=res[:], in0=acc[:], in1=bias[:, cols], op=ADD)
+                nc.sync.dma_start(out=rows[:, j, cols], in_=res[:])
+
+        READ_LAG = 1
+        FLIP_LAG = 3
+        PROJECT_LAG = 5
+        BIAS_STEP = 1
+        WO_STEP = 2
+        PROJECT_RUN = 2
+        for t in range(UNITS + PROJECT_LAG):
+            if t == BIAS_STEP:
+                spread_bias()
+            if 0 <= t - WO_STEP < C_HALVES * PASSES:
+                half, g = divmod(t - WO_STEP, PASSES)
+                prepare_wo(half, g)
+            if t < UNITS:
+                transpose_q(t)
+            if t == 0:
+                transpose_k_sum()
+            if t < UNITS and t % CHUNKS == 0:
+                transpose_vk(t // CHUNKS)
+            if 0 <= t - FLIP_LAG < UNITS:
+                transpose_a(t - FLIP_LAG)
+            if 0 <= t - READ_LAG < UNITS:
+                read_out(t - READ_LAG)
+            if 0 <= t - FLIP_LAG < UNITS:
+                quantise_a(t - FLIP_LAG)
+            last = t - PROJECT_LAG
+            if 0 <= last < UNITS and last % PROJECT_RUN == PROJECT_RUN - 1:
+                for u in range(last - PROJECT_RUN + 1, last + 1):
+                    project(u)

@@ -26,6 +26,8 @@ C_HALVES = C // BANK
 READ = D + 1
 HEADS_PER_BANK = BANK // READ
 HS_BANKS = -(-H // HEADS_PER_BANK)
+HALF = D // 2
+HEADS_PER_PASS = H // PASSES
 VK_SLOT = 144
 
 FLOPS = 2 * B * S * E * C + 2 * B * H * S * D * (D + 1)
@@ -95,7 +97,12 @@ def tile_lineartransformerblock_pc_kernel(tc, q_feat, vk, k_sum, Wo, bo, out):
             flipped = psum.tile([P, H, D], BF16, tag="bank")
             for h in range(H):
                 nc.tensor.transpose(flipped[:, h, :], vk_sb[b][:, h, :], ident_bf[:])
-            nc.vector.tensor_copy(out=vkT[:, b * H : (b + 1) * H, 0:D], in_=flipped[:])
+            by_parity = flipped[:].rearrange("p h (q u e) -> p h u q e", u=2, e=2)
+            for u in range(2):
+                nc.vector.tensor_copy(
+                    out=vkT[:, b * H : (b + 1) * H, u * HALF : (u + 1) * HALF].rearrange("p h (q e) -> p h q e", e=2),
+                    in_=by_parity[:, :, u],
+                )
 
         wo_words = wo_sb[:].rearrange("p k e -> p (k e)").bitcast(F32)
         wo_grouped = keep.tile([P, PASSES * C * PACK], BF16, align_bytes=64)
@@ -166,18 +173,19 @@ def tile_lineartransformerblock_pc_kernel(tc, q_feat, vk, k_sum, Wo, bo, out):
             rden = work.tile([P, H], F32, tag="rden")
             nc.vector.reciprocal(out=rden[:], in_=den[:])
             a_u = work.tile([P, E], BF16, tag="a")
+            by_head = a_u[:].rearrange("p (g u k r) -> p g k u r", g=PASSES, u=2, k=HEADS_PER_PASS)
             first_heads = banks[0][:, 0 : HEADS_PER_BANK * READ].rearrange("p (k r) -> p k r", r=READ)
             nc.vector.tensor_tensor(
-                out=a_u[:, 0 : HEADS_PER_BANK * D].rearrange("p (k n) -> p k n", n=D),
-                in0=first_heads[:, :, 0:D],
-                in1=rden[:, 0:HEADS_PER_BANK].unsqueeze(2).to_broadcast([P, HEADS_PER_BANK, D]),
+                out=by_head[:, 0, 0:HEADS_PER_BANK],
+                in0=first_heads[:, :, 0:D].rearrange("p k (u r) -> p k u r", u=2),
+                in1=rden[:, 0:HEADS_PER_BANK].unsqueeze(2).unsqueeze(3).to_broadcast([P, HEADS_PER_BANK, 2, HALF]),
                 op=MULT,
             )
             for h in range(HEADS_PER_BANK, H):
                 k, slot = divmod(h, HEADS_PER_BANK)
                 nc.scalar.activation(
-                    out=a_u[:, h * D : (h + 1) * D],
-                    in_=banks[k][:, slot * READ : slot * READ + D],
+                    out=by_head[:, h // HEADS_PER_PASS, h % HEADS_PER_PASS],
+                    in_=banks[k][:, slot * READ : slot * READ + D].rearrange("p (u r) -> p u r", u=2),
                     func=COPY,
                     scale=rden[:, h : h + 1],
                 )
@@ -187,10 +195,7 @@ def tile_lineartransformerblock_pc_kernel(tc, q_feat, vk, k_sum, Wo, bo, out):
             words = a_rows[u][:].bitcast(F32)
             flipped = psum.tile([P, BANK], F32, tag="bank")
             for w in range(E // 2 // P):
-                first = (w // 2) * 2 * P + w % 2
-                nc.tensor.transpose(
-                    flipped[:, w * P : (w + 1) * P], words[:, first : first + 2 * P - w % 2 : 2], ident_f32[:]
-                )
+                nc.tensor.transpose(flipped[:, w * P : (w + 1) * P], words[:, w * P : (w + 1) * P], ident_f32[:])
             grouped = work.tile([P, E], BF16, tag="grouped", align_bytes=64)
             nc.scalar.copy(
                 out=grouped[:].bitcast(F32).rearrange("p (g s u) -> p g s u", g=PASSES, u=2),

@@ -50,9 +50,17 @@ def tile_lineartransformerblock_pc_kernel(tc, q_feat, vk, k_sum, Wo, bo, out):
             q_sb.append(q_b)
         wo_sb = keep.tile([P, C // P, E], BF16)
 
-        def load_batch(b):
-            nc.sync.dma_start(out=q_sb[b][:], in_=q_feat[b].rearrange("h (p j) d -> p h (j d)", j=CHUNKS))
+        def load_q(b, first, last):
+            nc.sync.dma_start(
+                out=q_sb[b][:, first:last, :],
+                in_=q_feat[b, first:last].rearrange("h (p j) d -> p h (j d)", j=CHUNKS),
+            )
+
+        def load_vk(b):
             nc.sync.dma_start(out=vk_sb[b][:], in_=vk[b].rearrange("h n d -> n h d"))
+
+        def load_wo(first, last):
+            nc.sync.dma_start(out=wo_sb[:, first:last, :], in_=wo_rows[:, first:last, :])
 
         ks_rows = keep.tile([P, D], BF16)
         nc.vector.memset(ks_rows[32:64, :], 0.0)
@@ -61,14 +69,18 @@ def tile_lineartransformerblock_pc_kernel(tc, q_feat, vk, k_sum, Wo, bo, out):
         nc.vector.memset(bo_rows[:], 0.0)
 
         wo_rows = Wo.rearrange("(k p) e -> p k e", p=P)
-        load_batch(0)
+        half_rows = C // P // C_HALVES
+        load_wo(0, half_rows // 2)
+        load_wo(half_rows // 2, half_rows)
         nc.sync.dma_start(out=ks_rows[0 : B * H, :], in_=k_sum.rearrange("b h d -> (b h) d"))
+        load_vk(0)
+        load_q(0, 0, H // 2)
+        load_q(0, H // 2, H)
         nc.sync.dma_start(out=bo_rows[0:1, :], in_=bo.rearrange("(o c) -> o c", o=1))
-        for half in range(C_HALVES):
-            rows = slice(half * (BANK // P), (half + 1) * (BANK // P))
-            nc.sync.dma_start(out=wo_sb[:, rows, :], in_=wo_rows[:, rows, :])
+        load_wo(half_rows, 2 * half_rows)
         for b in range(1, B):
-            load_batch(b)
+            load_q(b, 0, H)
+            load_vk(b)
 
         ident_bf = keep.tile([P, P], BF16)
         make_identity(nc, ident_bf[:])
@@ -110,23 +122,24 @@ def tile_lineartransformerblock_pc_kernel(tc, q_feat, vk, k_sum, Wo, bo, out):
         wo_codes = keep.tile([P, PASSES * C], U32, align_bytes=64)
         wo_scales = keep.tile([P, PASSES * C], U8, align_bytes=64)
 
-        def prepare_wo(half, g):
-            for quarter in range(2):
-                c0 = half * BANK + quarter * 2 * P
-                flipped = psum.tile([P, 2, 2 * P], F32, tag="bank")
-                for u in range(2):
-                    for k in range(2):
-                        first = (c0 // P + k) * (E // 2) + 2 * g * P + u
-                        nc.tensor.transpose(
-                            flipped[:, u, k * P : (k + 1) * P],
-                            wo_words[:, first : first + 2 * P - u : 2],
-                            ident_f32[:],
-                        )
-                pairs = wo_pairs[:, g, c0 : c0 + 2 * P, :]
-                if quarter == 0:
-                    nc.scalar.copy(out=pairs, in_=flipped[:].rearrange("p u c -> p c u"))
-                else:
-                    nc.vector.tensor_copy(out=pairs, in_=flipped[:].rearrange("p u c -> p c u"))
+        def prepare_wo(quarter, g):
+            c0 = quarter * 2 * P
+            flipped = psum.tile([P, 2, 2 * P], F32, tag="bank")
+            for u in range(2):
+                for k in range(2):
+                    first = (c0 // P + k) * (E // 2) + 2 * g * P + u
+                    nc.tensor.transpose(
+                        flipped[:, u, k * P : (k + 1) * P],
+                        wo_words[:, first : first + 2 * P - u : 2],
+                        ident_f32[:],
+                    )
+            pairs = wo_pairs[:, g, c0 : c0 + 2 * P, :]
+            if quarter % 2 == 0:
+                nc.scalar.copy(out=pairs, in_=flipped[:].rearrange("p u c -> p c u"))
+            else:
+                nc.vector.tensor_copy(out=pairs, in_=flipped[:].rearrange("p u c -> p c u"))
+
+        def quantise_wo(half, g):
             first = g * C + half * BANK
             nc.vector.quantize_mx(
                 out=wo_codes[:, first : first + BANK].bitcast(FP8X4),
@@ -140,6 +153,23 @@ def tile_lineartransformerblock_pc_kernel(tc, q_feat, vk, k_sum, Wo, bo, out):
         a_codes = {}
         a_scales = {}
 
+        qT_first = keep.tile([P, CHUNKS, H, P], BF16)
+
+        def transpose_first_q(part, j):
+            heads = slice(part * H // 2, (part + 1) * H // 2)
+            flipped = psum.tile([P, 2, H // 2, P], BF16, tag="bank")
+            for i in range(2):
+                for h in range(H // 2):
+                    nc.tensor.transpose(
+                        flipped[:, i, h, :],
+                        q_sb[0][:, part * H // 2 + h, (j + i) * D : (j + i + 1) * D],
+                        ident_bf[:],
+                    )
+            if j == 0:
+                nc.scalar.copy(out=qT_first[:, j : j + 2, heads, :], in_=flipped[:])
+            else:
+                nc.vector.tensor_copy(out=qT_first[:, j : j + 2, heads, :], in_=flipped[:])
+
         def transpose_q(u):
             b, j = divmod(u, CHUNKS)
             flipped = psum.tile([P, H, P], BF16, tag="bank")
@@ -147,7 +177,7 @@ def tile_lineartransformerblock_pc_kernel(tc, q_feat, vk, k_sum, Wo, bo, out):
                 nc.tensor.transpose(flipped[:, h, :], q_sb[b][:, h, j * D : (j + 1) * D], ident_bf[:])
             qT_u = work.tile([P, H, P], BF16, tag="qT")
             nc.scalar.copy(out=qT_u[:], in_=flipped[:])
-            qT[u] = qT_u
+            qT[u] = qT_u[:]
 
         def read_out(u):
             b = u // CHUNKS
@@ -228,34 +258,45 @@ def tile_lineartransformerblock_pc_kernel(tc, q_feat, vk, k_sum, Wo, bo, out):
                         stop=(g == PASSES - 1),
                     )
                 cols = slice(half * BANK, (half + 1) * BANK)
-                res = work.tile([P, BANK], F32, tag="res", bufs=6)
+                res = work.tile([P, BANK], F32, tag="res", bufs=12)
                 nc.vector.tensor_tensor(out=res[:], in0=acc[:], in1=bias[:, cols], op=ADD)
                 nc.sync.dma_start(out=rows[:, j, cols], in_=res[:])
 
-        READ_LAG = 1
-        FLIP_LAG = 3
-        PROJECT_LAG = 5
-        BIAS_STEP = 1
-        WO_STEP = 2
+        for quarter in range(2):
+            for g in range(PASSES):
+                prepare_wo(quarter, g)
+        for g in range(PASSES):
+            quantise_wo(0, g)
+        transpose_k_sum()
+        transpose_vk(0)
+        for part in range(2):
+            for j in range(0, CHUNKS, 2):
+                transpose_first_q(part, j)
+        for j in range(CHUNKS):
+            qT[j] = qT_first[:, j]
+
+        Q_LEAD = 1
+        FLIP_LAG = 2
+        PROJECT_LAG = 4
         PROJECT_RUN = 2
         for t in range(UNITS + PROJECT_LAG):
-            if t == BIAS_STEP:
-                spread_bias()
-            if 0 <= t - WO_STEP < C_HALVES * PASSES:
-                half, g = divmod(t - WO_STEP, PASSES)
-                prepare_wo(half, g)
-            if t < UNITS:
-                transpose_q(t)
-            if t == 0:
-                transpose_k_sum()
-            if t < UNITS and t % CHUNKS == 0:
-                transpose_vk(t // CHUNKS)
+            if CHUNKS <= t + Q_LEAD < UNITS:
+                transpose_q(t + Q_LEAD)
+                if (t + Q_LEAD) % CHUNKS == 0:
+                    transpose_vk((t + Q_LEAD) // CHUNKS)
             if 0 <= t - FLIP_LAG < UNITS:
                 transpose_a(t - FLIP_LAG)
-            if 0 <= t - READ_LAG < UNITS:
-                read_out(t - READ_LAG)
+            if t < UNITS:
+                read_out(t)
             if 0 <= t - FLIP_LAG < UNITS:
                 quantise_a(t - FLIP_LAG)
+            if t in (2, 4):
+                quantise_wo(1, t // 2 - 1)
+            if t == 0:
+                spread_bias()
+            if t < CHUNKS:
+                g, quarter = divmod(t, 2)
+                prepare_wo(2 + quarter, g)
             last = t - PROJECT_LAG
             if 0 <= last < UNITS and last % PROJECT_RUN == PROJECT_RUN - 1:
                 for u in range(last - PROJECT_RUN + 1, last + 1):

@@ -62,6 +62,10 @@ def tile_lineartransformerblock_pc_kernel(tc, q_feat, vk, k_sum, Wo, bo, out):
         def load_wo(first, last):
             nc.sync.dma_start(out=wo_sb[:, first:last, :], in_=wo_rows[:, first:last, :])
 
+        ones = keep.tile([P, P], BF16)
+        nc.vector.memset(ones[:], 1.0)
+        warm_rhs = keep.tile([P, BANK], BF16)
+        nc.vector.memset(warm_rhs[:], 0.0)
         ks_rows = keep.tile([P, D], BF16)
         nc.vector.memset(ks_rows[32:64, :], 0.0)
         nc.vector.memset(ks_rows[64:128, :], 0.0)
@@ -70,13 +74,13 @@ def tile_lineartransformerblock_pc_kernel(tc, q_feat, vk, k_sum, Wo, bo, out):
 
         wo_rows = Wo.rearrange("(k p) e -> p k e", p=P)
         half_rows = C // P // C_HALVES
+        nc.scalar.dma_start(out=bo_rows[0:1, :], in_=bo.rearrange("(o c) -> o c", o=1))
+        nc.scalar.dma_start(out=ks_rows[0 : B * H, :], in_=k_sum.rearrange("b h d -> (b h) d"))
         load_wo(0, half_rows // 2)
         load_wo(half_rows // 2, half_rows)
-        nc.sync.dma_start(out=ks_rows[0 : B * H, :], in_=k_sum.rearrange("b h d -> (b h) d"))
         load_vk(0)
         load_q(0, 0, H // 2)
         load_q(0, H // 2, H)
-        nc.sync.dma_start(out=bo_rows[0:1, :], in_=bo.rearrange("(o c) -> o c", o=1))
         load_wo(half_rows, 2 * half_rows)
         for b in range(1, B):
             load_q(b, 0, H)
@@ -86,8 +90,11 @@ def tile_lineartransformerblock_pc_kernel(tc, q_feat, vk, k_sum, Wo, bo, out):
         make_identity(nc, ident_bf[:])
         ident_f32 = keep.tile([P, P], F32)
         make_identity(nc, ident_f32[:])
-        ones = keep.tile([P, P], BF16)
-        nc.vector.memset(ones[:], 1.0)
+
+        def keep_warm(passes):
+            unread = psum.tile([P, BANK], F32, tag="bank")
+            for k in range(passes):
+                nc.tensor.matmul(out=unread[:], lhsT=ones[:], rhs=warm_rhs[:], start=True, stop=True)
 
         bias = keep.tile([P, C], F32)
 
@@ -262,16 +269,21 @@ def tile_lineartransformerblock_pc_kernel(tc, q_feat, vk, k_sum, Wo, bo, out):
                 nc.vector.tensor_tensor(out=res[:], in0=acc[:], in1=bias[:, cols], op=ADD)
                 nc.sync.dma_start(out=rows[:, j, cols], in_=res[:])
 
+        keep_warm(4)
+        spread_bias()
+        transpose_k_sum()
         for quarter in range(2):
             for g in range(PASSES):
                 prepare_wo(quarter, g)
+            keep_warm(1)
         for g in range(PASSES):
             quantise_wo(0, g)
-        transpose_k_sum()
         transpose_vk(0)
+        keep_warm(1)
         for part in range(2):
             for j in range(0, CHUNKS, 2):
                 transpose_first_q(part, j)
+                keep_warm(1)
         for j in range(CHUNKS):
             qT[j] = qT_first[:, j]
 
@@ -292,8 +304,6 @@ def tile_lineartransformerblock_pc_kernel(tc, q_feat, vk, k_sum, Wo, bo, out):
                 quantise_a(t - FLIP_LAG)
             if t in (2, 4):
                 quantise_wo(1, t // 2 - 1)
-            if t == 0:
-                spread_bias()
             if t < CHUNKS:
                 g, quarter = divmod(t, 2)
                 prepare_wo(2 + quarter, g)

@@ -70,14 +70,14 @@ def tile_lineartransformerblock_pc_kernel(tc, q_feat, vk, k_sum, Wo, bo, out):
         nc.vector.memset(ks_rows[32:64, :], 0.0)
         nc.vector.memset(ks_rows[64:128, :], 0.0)
         bo_rows = keep.tile([P, C], BF16)
-        nc.vector.memset(bo_rows[:], 0.0)
+        nc.gpsimd.memset(bo_rows[:], 0.0)
 
         wo_rows = Wo.rearrange("(k p) e -> p k e", p=P)
         half_rows = C // P // C_HALVES
-        nc.scalar.dma_start(out=bo_rows[0:1, :], in_=bo.rearrange("(o c) -> o c", o=1))
-        nc.scalar.dma_start(out=ks_rows[0 : B * H, :], in_=k_sum.rearrange("b h d -> (b h) d"))
+        nc.sync.dma_start(out=ks_rows[0 : B * H, :], in_=k_sum.rearrange("b h d -> (b h) d"))
         load_wo(0, half_rows // 2)
         load_wo(half_rows // 2, half_rows)
+        nc.sync.dma_start(out=bo_rows[0:1, :], in_=bo.rearrange("(o c) -> o c", o=1))
         load_vk(0)
         load_q(0, 0, H // 2)
         load_q(0, H // 2, H)
@@ -269,17 +269,17 @@ def tile_lineartransformerblock_pc_kernel(tc, q_feat, vk, k_sum, Wo, bo, out):
                 nc.vector.tensor_tensor(out=res[:], in0=acc[:], in1=bias[:, cols], op=ADD)
                 nc.sync.dma_start(out=rows[:, j, cols], in_=res[:])
 
-        keep_warm(4)
-        spread_bias()
-        transpose_k_sum()
+        keep_warm(5)
         for quarter in range(2):
             for g in range(PASSES):
                 prepare_wo(quarter, g)
-            keep_warm(1)
+            if quarter == 0:
+                keep_warm(1)
+                transpose_k_sum()
         for g in range(PASSES):
             quantise_wo(0, g)
         transpose_vk(0)
-        keep_warm(1)
+        spread_bias()
         for part in range(2):
             for j in range(0, CHUNKS, 2):
                 transpose_first_q(part, j)

@@ -64,7 +64,7 @@ def tile_lineartransformerblock_pc_kernel(tc, q_feat, vk, k_sum, Wo, bo, out):
 
         ones = keep.tile([P, P], BF16)
         nc.vector.memset(ones[:], 1.0)
-        warm_rhs = keep.tile([P, BANK], BF16)
+        warm_rhs = keep.tile([P, P], F32)
         nc.vector.memset(warm_rhs[:], 0.0)
         ks_rows = keep.tile([P, D], BF16)
         nc.vector.memset(ks_rows[32:64, :], 0.0)
@@ -92,9 +92,9 @@ def tile_lineartransformerblock_pc_kernel(tc, q_feat, vk, k_sum, Wo, bo, out):
         make_identity(nc, ident_f32[:])
 
         def keep_warm(passes):
-            unread = psum.tile([P, BANK], F32, tag="bank")
+            unread = psum.tile([P, P], F32, tag="bank")
             for k in range(passes):
-                nc.tensor.matmul(out=unread[:], lhsT=ones[:], rhs=warm_rhs[:], start=True, stop=True)
+                nc.tensor.matmul(out=unread[:], lhsT=warm_rhs[:], rhs=warm_rhs[:], start=True, stop=True)
 
         bias = keep.tile([P, C], F32)
 
@@ -115,7 +115,10 @@ def tile_lineartransformerblock_pc_kernel(tc, q_feat, vk, k_sum, Wo, bo, out):
         def transpose_vk(b):
             flipped = psum.tile([P, H, D], BF16, tag="bank")
             for h in range(H):
-                nc.tensor.transpose(flipped[:, h, :], vk_sb[b][:, h, :], ident_bf[:])
+                if b == 0:
+                    nc.tensor.matmul(out=flipped[:, h, :], lhsT=vk_sb[b][:, h, :], rhs=ident_bf[:], start=True, stop=True)
+                else:
+                    nc.tensor.transpose(flipped[:, h, :], vk_sb[b][:, h, :], ident_bf[:])
             by_parity = flipped[:].rearrange("p h (q u e) -> p h u q e", u=2, e=2)
             for u in range(2):
                 nc.vector.tensor_copy(
@@ -167,10 +170,12 @@ def tile_lineartransformerblock_pc_kernel(tc, q_feat, vk, k_sum, Wo, bo, out):
             flipped = psum.tile([P, 2, H // 2, P], BF16, tag="bank")
             for i in range(2):
                 for h in range(H // 2):
-                    nc.tensor.transpose(
-                        flipped[:, i, h, :],
-                        q_sb[0][:, part * H // 2 + h, (j + i) * D : (j + i + 1) * D],
-                        ident_bf[:],
+                    nc.tensor.matmul(
+                        out=flipped[:, i, h, :],
+                        lhsT=q_sb[0][:, part * H // 2 + h, (j + i) * D : (j + i + 1) * D],
+                        rhs=ident_bf[:],
+                        start=True,
+                        stop=True,
                     )
             if j == 0:
                 nc.scalar.copy(out=qT_first[:, j : j + 2, heads, :], in_=flipped[:])
@@ -181,7 +186,10 @@ def tile_lineartransformerblock_pc_kernel(tc, q_feat, vk, k_sum, Wo, bo, out):
             b, j = divmod(u, CHUNKS)
             flipped = psum.tile([P, H, P], BF16, tag="bank")
             for h in range(H):
-                nc.tensor.transpose(flipped[:, h, :], q_sb[b][:, h, j * D : (j + 1) * D], ident_bf[:])
+                if u < 5:
+                    nc.tensor.matmul(out=flipped[:, h, :], lhsT=q_sb[b][:, h, j * D : (j + 1) * D], rhs=ident_bf[:], start=True, stop=True)
+                else:
+                    nc.tensor.transpose(flipped[:, h, :], q_sb[b][:, h, j * D : (j + 1) * D], ident_bf[:])
             qT_u = work.tile([P, H, P], BF16, tag="qT")
             nc.scalar.copy(out=qT_u[:], in_=flipped[:])
             qT[u] = qT_u[:]
@@ -269,12 +277,12 @@ def tile_lineartransformerblock_pc_kernel(tc, q_feat, vk, k_sum, Wo, bo, out):
                 nc.vector.tensor_tensor(out=res[:], in0=acc[:], in1=bias[:, cols], op=ADD)
                 nc.sync.dma_start(out=rows[:, j, cols], in_=res[:])
 
-        keep_warm(5)
+        keep_warm(6)
         for quarter in range(2):
             for g in range(PASSES):
                 prepare_wo(quarter, g)
+            keep_warm(2 - quarter)
             if quarter == 0:
-                keep_warm(1)
                 transpose_k_sum()
         for g in range(PASSES):
             quantise_wo(0, g)
@@ -283,7 +291,6 @@ def tile_lineartransformerblock_pc_kernel(tc, q_feat, vk, k_sum, Wo, bo, out):
         for part in range(2):
             for j in range(0, CHUNKS, 2):
                 transpose_first_q(part, j)
-                keep_warm(1)
         for j in range(CHUNKS):
             qT[j] = qT_first[:, j]
 
@@ -292,12 +299,12 @@ def tile_lineartransformerblock_pc_kernel(tc, q_feat, vk, k_sum, Wo, bo, out):
         PROJECT_LAG = 4
         PROJECT_RUN = 2
         for t in range(UNITS + PROJECT_LAG):
+            if 0 <= t - FLIP_LAG < UNITS:
+                transpose_a(t - FLIP_LAG)
             if CHUNKS <= t + Q_LEAD < UNITS:
                 transpose_q(t + Q_LEAD)
                 if (t + Q_LEAD) % CHUNKS == 0:
                     transpose_vk((t + Q_LEAD) // CHUNKS)
-            if 0 <= t - FLIP_LAG < UNITS:
-                transpose_a(t - FLIP_LAG)
             if t < UNITS:
                 read_out(t)
             if 0 <= t - FLIP_LAG < UNITS:

@@ -23,7 +23,7 @@ BANK = 512
 CHUNKS = S // P
 UNITS = B * CHUNKS
 C_HALVES = C // BANK
-READ = D + 1
+READ = D + 2
 HEADS_PER_BANK = BANK // READ
 HS_BANKS = -(-H // HEADS_PER_BANK)
 HALF = D // 2
@@ -106,6 +106,8 @@ def tile_lineartransformerblock_pc_kernel(tc, q_feat, vk, k_sum, Wo, bo, out):
                 nc.vector.tensor_copy(out=bias[:, cols], in_=spread[:])
 
         vkT = keep.tile([P, B * H, VK_SLOT], BF16)
+
+        nc.vector.memset(vkT[:, :, D:READ], 0.0)
 
         def transpose_k_sum():
             ksT = psum.tile([P, P], BF16, tag="bank")
@@ -214,7 +216,7 @@ def tile_lineartransformerblock_pc_kernel(tc, q_feat, vk, k_sum, Wo, bo, out):
                 h0 = k * HEADS_PER_BANK
                 n = min(HEADS_PER_BANK, H - h0)
                 slots = banks[k][:, 0 : n * READ].rearrange("p (k r) -> p k r", r=READ)
-                nc.vector.tensor_scalar_add(out=den[:, h0 : h0 + n].unsqueeze(2), in0=slots[:, :, D:READ], scalar1=EPS)
+                nc.vector.tensor_scalar_add(out=den[:, h0 : h0 + n].unsqueeze(2), in0=slots[:, :, D : D + 1], scalar1=EPS)
             rden = work.tile([P, H], F32, tag="rden")
             nc.vector.reciprocal(out=rden[:], in_=den[:])
             a_u = work.tile([P, E], BF16, tag="a")

@@ -276,7 +276,11 @@ def tile_lineartransformerblock_pc_kernel(tc, q_feat, vk, k_sum, Wo, bo, out):
                     )
                 cols = slice(half * BANK, (half + 1) * BANK)
                 res = work.tile([P, BANK], F32, tag="res", bufs=12)
-                nc.vector.tensor_tensor(out=res[:], in0=acc[:], in1=bias[:, cols], op=ADD)
+                if u % 2 == 1 and half == 1 and u < UNITS - 1:
+                    nc.scalar.copy(out=res[:], in_=acc[:])
+                    nc.gpsimd.tensor_tensor(out=res[:], in0=res[:], in1=bias[:, cols], op=ADD)
+                else:
+                    nc.vector.tensor_tensor(out=res[:], in0=acc[:], in1=bias[:, cols], op=ADD)
                 nc.sync.dma_start(out=rows[:, j, cols], in_=res[:])
 
         keep_warm(6)

@@ -62,22 +62,18 @@ def tile_lineartransformerblock_pc_kernel(tc, q_feat, vk, k_sum, Wo, bo, out):
         def load_wo(first, last):
             nc.sync.dma_start(out=wo_sb[:, first:last, :], in_=wo_rows[:, first:last, :])
 
-        ones = keep.tile([P, P], BF16)
-        nc.vector.memset(ones[:], 1.0)
         warm_rhs = keep.tile([P, P], F32)
         nc.vector.memset(warm_rhs[:], 0.0)
         ks_rows = keep.tile([P, D], BF16)
         nc.vector.memset(ks_rows[32:64, :], 0.0)
         nc.vector.memset(ks_rows[64:128, :], 0.0)
-        bo_rows = keep.tile([P, C], BF16)
-        nc.gpsimd.memset(bo_rows[:], 0.0)
+        bias = keep.tile([P, C], BF16)
 
         wo_rows = Wo.rearrange("(k p) e -> p k e", p=P)
         half_rows = C // P // C_HALVES
         nc.sync.dma_start(out=ks_rows[0 : B * H, :], in_=k_sum.rearrange("b h d -> (b h) d"))
         load_wo(0, half_rows // 2)
         load_wo(half_rows // 2, half_rows)
-        nc.sync.dma_start(out=bo_rows[0:1, :], in_=bo.rearrange("(o c) -> o c", o=1))
         load_vk(0)
         load_q(0, 0, H // 2)
         load_q(0, H // 2, H)
@@ -85,6 +81,8 @@ def tile_lineartransformerblock_pc_kernel(tc, q_feat, vk, k_sum, Wo, bo, out):
         for b in range(1, B):
             load_q(b, 0, H)
             load_vk(b)
+            if b == 1:
+                nc.sync.dma_start(out=bias[:], in_=bo.partition_broadcast(P))
 
         ident_bf = keep.tile([P, P], BF16)
         make_identity(nc, ident_bf[:])
@@ -95,15 +93,6 @@ def tile_lineartransformerblock_pc_kernel(tc, q_feat, vk, k_sum, Wo, bo, out):
             unread = psum.tile([P, P], F32, tag="bank")
             for k in range(passes):
                 nc.tensor.matmul(out=unread[:], lhsT=warm_rhs[:], rhs=warm_rhs[:], start=True, stop=True)
-
-        bias = keep.tile([P, C], F32)
-
-        def spread_bias():
-            for half in range(C_HALVES):
-                cols = slice(half * BANK, (half + 1) * BANK)
-                spread = psum.tile([P, BANK], F32, tag="bank")
-                nc.tensor.matmul(out=spread[:], lhsT=ones[:], rhs=bo_rows[:, cols], start=True, stop=True)
-                nc.vector.tensor_copy(out=bias[:, cols], in_=spread[:])
 
         vkT = keep.tile([P, B * H, VK_SLOT], BF16)
 
@@ -260,11 +249,12 @@ def tile_lineartransformerblock_pc_kernel(tc, q_feat, vk, k_sum, Wo, bo, out):
         def project(u):
             b, j = divmod(u, CHUNKS)
             rows = out[b].rearrange("(p j) c -> p j c", j=CHUNKS)
-            for half in range(C_HALVES):
-                acc = psum.tile([P, BANK], F32, tag="bank")
+            width = BANK if u < UNITS - 1 else BANK // 2
+            for c0 in range(0, C, width):
+                acc = psum.tile([P, width], F32, tag="bank")
                 for g in range(PASSES):
                     tokens = slice(g * P, (g + 1) * P)
-                    cols = slice(g * C + half * BANK, g * C + (half + 1) * BANK)
+                    cols = slice(g * C + c0, g * C + c0 + width)
                     nc.tensor.matmul_mx(
                         out=acc[:],
                         lhsT=a_codes[u][:, tokens].bitcast(FP8X4),
@@ -274,9 +264,9 @@ def tile_lineartransformerblock_pc_kernel(tc, q_feat, vk, k_sum, Wo, bo, out):
                         start=(g == 0),
                         stop=(g == PASSES - 1),
                     )
-                cols = slice(half * BANK, (half + 1) * BANK)
-                res = work.tile([P, BANK], F32, tag="res", bufs=12)
-                if u % 2 == 1 and half == 1 and u < UNITS - 1:
+                cols = slice(c0, c0 + width)
+                res = work.tile([P, width], F32, tag="res", bufs=12)
+                if u % 2 == 1 and c0 > 0 and u < UNITS - 1:
                     nc.scalar.copy(out=res[:], in_=acc[:])
                     nc.gpsimd.tensor_tensor(out=res[:], in0=res[:], in1=bias[:, cols], op=ADD)
                 else:
@@ -293,7 +283,6 @@ def tile_lineartransformerblock_pc_kernel(tc, q_feat, vk, k_sum, Wo, bo, out):
         for g in range(PASSES):
             quantise_wo(0, g)
         transpose_vk(0)
-        spread_bias()
         for part in range(2):
             for j in range(0, CHUNKS, 2):
                 transpose_first_q(part, j)

@@ -120,8 +120,8 @@ def tile_lineartransformerblock_pc_kernel(tc, q_feat, vk, k_sum, Wo, bo, out):
         wo_words = wo_sb[:].rearrange("p k e -> p (k e)").bitcast(F32)
         wo_grouped = keep.tile([P, PASSES * C * PACK], BF16, align_bytes=64)
         wo_pairs = wo_grouped[:].bitcast(F32).rearrange("p (g c u) -> p g c u", g=PASSES, u=2)
-        wo_codes = keep.tile([P, PASSES * C], U32, align_bytes=64)
-        wo_scales = keep.tile([P, PASSES * C], U8, align_bytes=64)
+        wo_codes = keep.tile([P, PASSES * C], U32, align_bytes=256)
+        wo_scales = keep.tile([P, PASSES * C], U8, align_bytes=256)
 
         def prepare_wo(quarter, g):
             c0 = quarter * 2 * P
@@ -177,7 +177,7 @@ def tile_lineartransformerblock_pc_kernel(tc, q_feat, vk, k_sum, Wo, bo, out):
             b, j = divmod(u, CHUNKS)
             flipped = psum.tile([P, H, P], BF16, tag="bank")
             for h in range(H):
-                if u < 5:
+                if u < 6:
                     nc.tensor.matmul(out=flipped[:, h, :], lhsT=q_sb[b][:, h, j * D : (j + 1) * D], rhs=ident_bf[:], start=True, stop=True)
                 else:
                     nc.tensor.transpose(flipped[:, h, :], q_sb[b][:, h, j * D : (j + 1) * D], ident_bf[:])
@@ -240,38 +240,51 @@ def tile_lineartransformerblock_pc_kernel(tc, q_feat, vk, k_sum, Wo, bo, out):
             a_grouped[u] = grouped
 
         def quantise_a(u):
-            codes = work.tile([P, PASSES * P], U32, tag="codes", bufs=6, align_bytes=64)
-            scales = work.tile([P, PASSES * P], U8, tag="scales", bufs=6, align_bytes=64)
+            codes = work.tile([P, PASSES * P], U32, tag="codes", bufs=6, align_bytes=256)
+            scales = work.tile([P, PASSES * P], U8, tag="scales", bufs=6, align_bytes=256)
             nc.vector.quantize_mx(out=codes[:].bitcast(FP8X4), scales=scales[:], in_=a_grouped[u][:])
             a_codes[u] = codes
             a_scales[u] = scales
 
-        def project(u):
-            b, j = divmod(u, CHUNKS)
+        PROJECT_RUN = 2
+
+        def project_columns(u, c0, width, res):
+            acc = psum.tile([P, width], F32, tag="bank")
+            for g in range(PASSES):
+                tokens = slice(g * P, (g + 1) * P)
+                cols = slice(g * C + c0, g * C + c0 + width)
+                nc.tensor.matmul_mx(
+                    out=acc[:],
+                    lhsT=a_codes[u][:, tokens].bitcast(FP8X4),
+                    lhsT_scale=a_scales[u][:, tokens],
+                    rhs=wo_codes[:, cols].bitcast(FP8X4),
+                    rhs_scale=wo_scales[:, cols],
+                    start=(g == 0),
+                    stop=(g == PASSES - 1),
+                )
+            cols = slice(c0, c0 + width)
+            if u % 2 == 1 and c0 > 0 and u < UNITS - 1:
+                nc.scalar.copy(out=res, in_=acc[:])
+                nc.gpsimd.tensor_tensor(out=res, in0=res, in1=bias[:, cols], op=ADD)
+            else:
+                nc.vector.tensor_tensor(out=res, in0=acc[:], in1=bias[:, cols], op=ADD)
+
+        def project(first):
+            b, j = divmod(first, CHUNKS)
             rows = out[b].rearrange("(p j) c -> p j c", j=CHUNKS)
-            width = BANK if u < UNITS - 1 else BANK // 2
-            for c0 in range(0, C, width):
-                acc = psum.tile([P, width], F32, tag="bank")
-                for g in range(PASSES):
-                    tokens = slice(g * P, (g + 1) * P)
-                    cols = slice(g * C + c0, g * C + c0 + width)
-                    nc.tensor.matmul_mx(
-                        out=acc[:],
-                        lhsT=a_codes[u][:, tokens].bitcast(FP8X4),
-                        lhsT_scale=a_scales[u][:, tokens],
-                        rhs=wo_codes[:, cols].bitcast(FP8X4),
-                        rhs_scale=wo_scales[:, cols],
-                        start=(g == 0),
-                        stop=(g == PASSES - 1),
-                    )
-                cols = slice(c0, c0 + width)
-                res = work.tile([P, width], F32, tag="res", bufs=12)
-                if u % 2 == 1 and c0 > 0 and u < UNITS - 1:
-                    nc.scalar.copy(out=res[:], in_=acc[:])
-                    nc.gpsimd.tensor_tensor(out=res[:], in0=res[:], in1=bias[:, cols], op=ADD)
-                else:
-                    nc.vector.tensor_tensor(out=res[:], in0=acc[:], in1=bias[:, cols], op=ADD)
-                nc.sync.dma_start(out=rows[:, j, cols], in_=res[:])
+            if first < UNITS - 3 * PROJECT_RUN:
+                res = work.tile([P, PROJECT_RUN, C], F32, tag="res")
+                for i in range(PROJECT_RUN):
+                    for c0 in range(0, C, BANK):
+                        project_columns(first + i, c0, BANK, res[:, i, c0 : c0 + BANK])
+                nc.sync.dma_start(out=rows[:, j : j + PROJECT_RUN, :], in_=res[:])
+            else:
+                for i in range(PROJECT_RUN):
+                    width = BANK if first + i < UNITS - 1 else BANK // 2
+                    for c0 in range(0, C, width):
+                        last = work.tile([P, width], F32, tag="last", bufs=8)
+                        project_columns(first + i, c0, width, last[:])
+                        nc.sync.dma_start(out=rows[:, j + i, c0 : c0 + width], in_=last[:])
 
         keep_warm(6)
         for quarter in range(2):
@@ -292,7 +305,6 @@ def tile_lineartransformerblock_pc_kernel(tc, q_feat, vk, k_sum, Wo, bo, out):
         Q_LEAD = 1
         FLIP_LAG = 2
         PROJECT_LAG = 4
-        PROJECT_RUN = 2
         for t in range(UNITS + PROJECT_LAG):
             if 0 <= t - FLIP_LAG < UNITS:
                 transpose_a(t - FLIP_LAG)
@@ -311,5 +323,4 @@ def tile_lineartransformerblock_pc_kernel(tc, q_feat, vk, k_sum, Wo, bo, out):
                 prepare_wo(2 + quarter, g)
             last = t - PROJECT_LAG
             if 0 <= last < UNITS and last % PROJECT_RUN == PROJECT_RUN - 1:
-                for u in range(last - PROJECT_RUN + 1, last + 1):
-                    project(u)
+                project(last - PROJECT_RUN + 1)

from contextlib import ExitStack

import concourse.mybir as mybir
from concourse.masks import make_identity

BF16 = mybir.dt.bfloat16
F32 = mybir.dt.float32
U32 = mybir.dt.uint32
U8 = mybir.dt.uint8
FP8X4 = mybir.dt.float8_e4m3fn_x4
COPY = mybir.ActivationFunctionType.Copy
ADD = mybir.AluOpType.add
MULT = mybir.AluOpType.mult

B, H, S, D, C = 4, 8, 512, 128, 1024
E = H * D
EPS = 1e-15
P = 128
PACK = 4
K_PASS = P * PACK
PASSES = E // K_PASS
BANK = 512
CHUNKS = S // P
UNITS = B * CHUNKS
C_HALVES = C // BANK
READ = D + 2
HEADS_PER_BANK = BANK // READ
HS_BANKS = -(-H // HEADS_PER_BANK)
HALF = D // 2
HEADS_PER_PASS = H // PASSES
VK_SLOT = 144

FLOPS = 2 * B * S * E * C + 2 * B * H * S * D * (D + 1)


def tile_lineartransformerblock_pc_kernel(tc, q_feat, vk, k_sum, Wo, bo, out):
    nc = tc.nc
    with ExitStack() as ctx:
        ctx.enter_context(tc.manual_schedule())
        keep = ctx.enter_context(tc.tile_pool(name="keep", bufs=1))
        work = ctx.enter_context(tc.tile_pool(name="work", bufs=3))
        psum = ctx.enter_context(tc.psum_pool(name="psum", bufs=8))

        vk_sb = []
        q_sb = []
        for b in range(B):
            vk_b = keep.tile([P, H, D], BF16, name="vk%d" % b)
            q_b = keep.tile([P, H, CHUNKS * D], BF16, name="q%d" % b)
            vk_sb.append(vk_b)
            q_sb.append(q_b)
        wo_sb = keep.tile([P, C // P, E], BF16)

        def load_q(b, first, last):
            nc.sync.dma_start(
                out=q_sb[b][:, first:last, :],
                in_=q_feat[b, first:last].rearrange("h (p j) d -> p h (j d)", j=CHUNKS),
            )

        def load_vk(b):
            nc.sync.dma_start(out=vk_sb[b][:], in_=vk[b].rearrange("h n d -> n h d"))

        def load_wo(first, last):
            nc.sync.dma_start(out=wo_sb[:, first:last, :], in_=wo_rows[:, first:last, :])

        warm_rhs = keep.tile([P, P], F32)
        nc.vector.memset(warm_rhs[:], 0.0)
        ks_rows = keep.tile([P, D], BF16)
        nc.vector.memset(ks_rows[32:64, :], 0.0)
        nc.vector.memset(ks_rows[64:128, :], 0.0)
        bias = keep.tile([P, C], BF16)

        wo_rows = Wo.rearrange("(k p) e -> p k e", p=P)
        half_rows = C // P // C_HALVES
        nc.sync.dma_start(out=ks_rows[0 : B * H, :], in_=k_sum.rearrange("b h d -> (b h) d"))
        load_wo(0, half_rows // 2)
        load_wo(half_rows // 2, half_rows)
        load_vk(0)
        load_q(0, 0, H // 2)
        load_q(0, H // 2, H)
        load_wo(half_rows, 2 * half_rows)
        for b in range(1, B):
            load_q(b, 0, H)
            load_vk(b)
            if b == 1:
                nc.sync.dma_start(out=bias[:], in_=bo.partition_broadcast(P))

        ident_bf = keep.tile([P, P], BF16)
        make_identity(nc, ident_bf[:])
        ident_f32 = keep.tile([P, P], F32)
        make_identity(nc, ident_f32[:])

        def keep_warm(passes):
            unread = psum.tile([P, P], F32, tag="bank")
            for k in range(passes):
                nc.tensor.matmul(out=unread[:], lhsT=warm_rhs[:], rhs=warm_rhs[:], start=True, stop=True)

        vkT = keep.tile([P, B * H, VK_SLOT], BF16)

        nc.vector.memset(vkT[:, :, D:READ], 0.0)

        def transpose_k_sum():
            ksT = psum.tile([P, P], BF16, tag="bank")
            nc.tensor.transpose(ksT[:], ks_rows[:], ident_bf[:])
            nc.vector.tensor_copy(out=vkT[:, :, D : D + 1], in_=ksT[:, 0 : B * H].unsqueeze(2))

        def transpose_vk(b):
            flipped = psum.tile([P, H, D], BF16, tag="bank")
            for h in range(H):
                if b == 0:
                    nc.tensor.matmul(out=flipped[:, h, :], lhsT=vk_sb[b][:, h, :], rhs=ident_bf[:], start=True, stop=True)
                else:
                    nc.tensor.transpose(flipped[:, h, :], vk_sb[b][:, h, :], ident_bf[:])
            by_parity = flipped[:].rearrange("p h (q u e) -> p h u q e", u=2, e=2)
            for u in range(2):
                nc.vector.tensor_copy(
                    out=vkT[:, b * H : (b + 1) * H, u * HALF : (u + 1) * HALF].rearrange("p h (q e) -> p h q e", e=2),
                    in_=by_parity[:, :, u],
                )

        wo_words = wo_sb[:].rearrange("p k e -> p (k e)").bitcast(F32)
        wo_grouped = keep.tile([P, PASSES * C * PACK], BF16, align_bytes=64)
        wo_pairs = wo_grouped[:].bitcast(F32).rearrange("p (g c u) -> p g c u", g=PASSES, u=2)
        wo_codes = keep.tile([P, PASSES * C], U32, align_bytes=256)
        wo_scales = keep.tile([P, PASSES * C], U8, align_bytes=256)

        def prepare_wo(quarter, g):
            c0 = quarter * 2 * P
            flipped = psum.tile([P, 2, 2 * P], F32, tag="bank")
            for u in range(2):
                for k in range(2):
                    first = (c0 // P + k) * (E // 2) + 2 * g * P + u
                    nc.tensor.transpose(
                        flipped[:, u, k * P : (k + 1) * P],
                        wo_words[:, first : first + 2 * P - u : 2],
                        ident_f32[:],
                    )
            pairs = wo_pairs[:, g, c0 : c0 + 2 * P, :]
            if quarter % 2 == 0:
                nc.scalar.copy(out=pairs, in_=flipped[:].rearrange("p u c -> p c u"))
            else:
                nc.vector.tensor_copy(out=pairs, in_=flipped[:].rearrange("p u c -> p c u"))

        def quantise_wo(half, g):
            first = g * C + half * BANK
            nc.vector.quantize_mx(
                out=wo_codes[:, first : first + BANK].bitcast(FP8X4),
                scales=wo_scales[:, first : first + BANK],
                in_=wo_grouped[:, first * PACK : (first + BANK) * PACK],
            )

        qT = {}
        a_rows = {}
        a_grouped = {}
        a_codes = {}
        a_scales = {}

        qT_first = keep.tile([P, CHUNKS, H, P], BF16)

        def transpose_first_q(part, j):
            heads = slice(part * H // 2, (part + 1) * H // 2)
            flipped = psum.tile([P, 2, H // 2, P], BF16, tag="bank")
            for i in range(2):
                for h in range(H // 2):
                    nc.tensor.matmul(
                        out=flipped[:, i, h, :],
                        lhsT=q_sb[0][:, part * H // 2 + h, (j + i) * D : (j + i + 1) * D],
                        rhs=ident_bf[:],
                        start=True,
                        stop=True,
                    )
            if j == 0:
                nc.scalar.copy(out=qT_first[:, j : j + 2, heads, :], in_=flipped[:])
            else:
                nc.vector.tensor_copy(out=qT_first[:, j : j + 2, heads, :], in_=flipped[:])

        def transpose_q(u):
            b, j = divmod(u, CHUNKS)
            flipped = psum.tile([P, H, P], BF16, tag="bank")
            for h in range(H):
                if u < 6:
                    nc.tensor.matmul(out=flipped[:, h, :], lhsT=q_sb[b][:, h, j * D : (j + 1) * D], rhs=ident_bf[:], start=True, stop=True)
                else:
                    nc.tensor.transpose(flipped[:, h, :], q_sb[b][:, h, j * D : (j + 1) * D], ident_bf[:])
            qT_u = work.tile([P, H, P], BF16, tag="qT")
            nc.scalar.copy(out=qT_u[:], in_=flipped[:])
            qT[u] = qT_u[:]

        def read_out(u):
            b = u // CHUNKS
            banks = []
            for k in range(HS_BANKS):
                bank = psum.tile([P, BANK], F32, tag="bank")
                banks.append(bank)
            for h in range(H):
                k, slot = divmod(h, HEADS_PER_BANK)
                nc.tensor.matmul(
                    out=banks[k][:, slot * READ : (slot + 1) * READ],
                    lhsT=qT[u][:, h, :],
                    rhs=vkT[:, b * H + h, 0:READ],
                    start=True,
                    stop=True,
                )
            den = work.tile([P, H], F32, tag="den")
            for k in range(HS_BANKS):
                h0 = k * HEADS_PER_BANK
                n = min(HEADS_PER_BANK, H - h0)
                slots = banks[k][:, 0 : n * READ].rearrange("p (k r) -> p k r", r=READ)
                nc.vector.tensor_scalar_add(out=den[:, h0 : h0 + n].unsqueeze(2), in0=slots[:, :, D : D + 1], scalar1=EPS)
            rden = work.tile([P, H], F32, tag="rden")
            nc.vector.reciprocal(out=rden[:], in_=den[:])
            a_u = work.tile([P, E], BF16, tag="a")
            by_head = a_u[:].rearrange("p (g u k r) -> p g k u r", g=PASSES, u=2, k=HEADS_PER_PASS)
            first_heads = banks[0][:, 0 : HEADS_PER_BANK * READ].rearrange("p (k r) -> p k r", r=READ)
            nc.vector.tensor_tensor(
                out=by_head[:, 0, 0:HEADS_PER_BANK],
                in0=first_heads[:, :, 0:D].rearrange("p k (u r) -> p k u r", u=2),
                in1=rden[:, 0:HEADS_PER_BANK].unsqueeze(2).unsqueeze(3).to_broadcast([P, HEADS_PER_BANK, 2, HALF]),
                op=MULT,
            )
            for h in range(HEADS_PER_BANK, H):
                k, slot = divmod(h, HEADS_PER_BANK)
                nc.scalar.activation(
                    out=by_head[:, h // HEADS_PER_PASS, h % HEADS_PER_PASS],
                    in_=banks[k][:, slot * READ : slot * READ + D].rearrange("p (u r) -> p u r", u=2),
                    func=COPY,
                    scale=rden[:, h : h + 1],
                )
            a_rows[u] = a_u

        def transpose_a(u):
            words = a_rows[u][:].bitcast(F32)
            flipped = psum.tile([P, BANK], F32, tag="bank")
            for w in range(E // 2 // P):
                nc.tensor.transpose(flipped[:, w * P : (w + 1) * P], words[:, w * P : (w + 1) * P], ident_f32[:])
            grouped = work.tile([P, E], BF16, tag="grouped", align_bytes=64)
            nc.scalar.copy(
                out=grouped[:].bitcast(F32).rearrange("p (g s u) -> p g s u", g=PASSES, u=2),
                in_=flipped[:].rearrange("p (g u s) -> p g s u", g=PASSES, u=2),
            )
            a_grouped[u] = grouped

        def quantise_a(u):
            codes = work.tile([P, PASSES * P], U32, tag="codes", bufs=6, align_bytes=256)
            scales = work.tile([P, PASSES * P], U8, tag="scales", bufs=6, align_bytes=256)
            nc.vector.quantize_mx(out=codes[:].bitcast(FP8X4), scales=scales[:], in_=a_grouped[u][:])
            a_codes[u] = codes
            a_scales[u] = scales

        PROJECT_RUN = 2

        def project_columns(u, c0, width, res):
            acc = psum.tile([P, width], F32, tag="bank")
            for g in range(PASSES):
                tokens = slice(g * P, (g + 1) * P)
                cols = slice(g * C + c0, g * C + c0 + width)
                nc.tensor.matmul_mx(
                    out=acc[:],
                    lhsT=a_codes[u][:, tokens].bitcast(FP8X4),
                    lhsT_scale=a_scales[u][:, tokens],
                    rhs=wo_codes[:, cols].bitcast(FP8X4),
                    rhs_scale=wo_scales[:, cols],
                    start=(g == 0),
                    stop=(g == PASSES - 1),
                )
            cols = slice(c0, c0 + width)
            if u % 2 == 1 and c0 > 0 and u < UNITS - 1:
                nc.scalar.copy(out=res, in_=acc[:])
                nc.gpsimd.tensor_tensor(out=res, in0=res, in1=bias[:, cols], op=ADD)
            else:
                nc.vector.tensor_tensor(out=res, in0=acc[:], in1=bias[:, cols], op=ADD)

        def project(first):
            b, j = divmod(first, CHUNKS)
            rows = out[b].rearrange("(p j) c -> p j c", j=CHUNKS)
            if first < UNITS - 3 * PROJECT_RUN:
                res = work.tile([P, PROJECT_RUN, C], F32, tag="res")
                for i in range(PROJECT_RUN):
                    for c0 in range(0, C, BANK):
                        project_columns(first + i, c0, BANK, res[:, i, c0 : c0 + BANK])
                nc.sync.dma_start(out=rows[:, j : j + PROJECT_RUN, :], in_=res[:])
            else:
                for i in range(PROJECT_RUN):
                    width = BANK if first + i < UNITS - 1 else BANK // 2
                    for c0 in range(0, C, width):
                        last = work.tile([P, width], F32, tag="last", bufs=8)
                        project_columns(first + i, c0, width, last[:])
                        nc.sync.dma_start(out=rows[:, j + i, c0 : c0 + width], in_=last[:])

        keep_warm(6)
        for quarter in range(2):
            for g in range(PASSES):
                prepare_wo(quarter, g)
            keep_warm(2 - quarter)
            if quarter == 0:
                transpose_k_sum()
        for g in range(PASSES):
            quantise_wo(0, g)
        transpose_vk(0)
        for part in range(2):
            for j in range(0, CHUNKS, 2):
                transpose_first_q(part, j)
        for j in range(CHUNKS):
            qT[j] = qT_first[:, j]

        Q_LEAD = 1
        FLIP_LAG = 2
        PROJECT_LAG = 4
        for t in range(UNITS + PROJECT_LAG):
            if 0 <= t - FLIP_LAG < UNITS:
                transpose_a(t - FLIP_LAG)
            if CHUNKS <= t + Q_LEAD < UNITS:
                transpose_q(t + Q_LEAD)
                if (t + Q_LEAD) % CHUNKS == 0:
                    transpose_vk((t + Q_LEAD) // CHUNKS)
            if t < UNITS:
                read_out(t)
            if 0 <= t - FLIP_LAG < UNITS:
                quantise_a(t - FLIP_LAG)
            if t in (2, 4):
                quantise_wo(1, t // 2 - 1)
            if t < CHUNKS:
                g, quarter = divmod(t, 2)
                prepare_wo(2 + quarter, g)
            last = t - PROJECT_LAG
            if 0 <= last < UNITS and last % PROJECT_RUN == PROJECT_RUN - 1:
                project(last - PROJECT_RUN + 1)
